import numpy as np
import ml_dtypes


def mxq(x, axis, fmt="e4m3"):
    dtype, down = {"e4m3": (ml_dtypes.float8_e4m3fn, 7), "e5m2": (ml_dtypes.float8_e5m2, 14)}[fmt]
    v = np.moveaxis(np.asarray(x, np.float32).astype(ml_dtypes.bfloat16).astype(np.float64), axis, -1)
    blocks = v.reshape(v.shape[:-1] + (-1, 32))
    amax = np.abs(blocks).max(-1, keepdims=True)
    byte = np.maximum(np.where(amax > 0, np.frexp(amax)[1] - 1 + 127, 0) - down, 1)
    scale = np.exp2(byte - 127.0)
    codes = (blocks / scale).astype(np.float32).astype(dtype).astype(np.float64)
    return np.moveaxis((codes * scale).reshape(v.shape), -1, axis)


WIDE = False


def mx_kscale(k):
    if not WIDE:
        return np.ones(k)
    levels = np.array([10, -10, 5, -5, 0])
    a = np.random.permutation(np.resize(levels, k // 512 * 4)).reshape(k // 512, 4)
    idx = np.arange(k)
    return np.exp2(a[idx // 512, idx % 128 // 32])


BF16 = ml_dtypes.bfloat16


def bf(x):
    return np.asarray(x, np.float32).astype(BF16)


def f64(x):
    return np.asarray(x).astype(np.float64)


B, C, H, W, K = 2, 256, 128, 128, 128
N = H * W
XS = 1.6 / C ** 0.25
CS = 0.4 / C ** 0.25


def setup_inputs():
    s = mx_kscale(N)
    z = 1.3 * np.random.standard_normal((B, N, K)) + np.random.standard_normal((1, 1, K))
    a = np.exp(z - z.max(axis=-1, keepdims=True))
    a = a / a.sum(axis=-1, keepdims=True)
    feat = XS * (np.random.standard_normal((B, N, C)) + 0.4 * np.random.standard_normal((1, 1, C)))
    return {'assign': bf(a * s[None, :, None]),
            'xp': bf(feat / s[None, :, None]),
            'codebook': bf(np.random.standard_normal((K, C)) * CS / s.mean())}


def reference(assign, xp, codebook):
    assign, xp, codebook = f64(assign), f64(xp), f64(codebook)
    a_sum = np.sum(assign, axis=1)
    e = (mxq(assign, 1, 'e4m3').transpose(0, 2, 1) @ mxq(xp, 1, 'e4m3')) - a_sum[:, :, None] * codebook[None]
    return e

@@ -1,0 +1,150 @@
+from contextlib import ExitStack
+
+import concourse.mybir as mybir
+
+BF16 = mybir.dt.bfloat16
+F32 = mybir.dt.float32
+U32 = mybir.dt.uint32
+U8 = mybir.dt.uint8
+FP8X4 = mybir.dt.float8_e4m3fn_x4
+MULT = mybir.AluOpType.mult
+ADD = mybir.AluOpType.add
+
+P = 128
+PACK = 4
+K_PASS = P * PACK
+
+IMAGES = 2
+PIXELS = 16384
+CODEWORDS = 128
+CHANNELS = 256
+
+PASSES = 4
+CHUNK_PIXELS = PASSES * K_PASS
+CHUNKS = PIXELS // CHUNK_PIXELS
+RUN = 4
+
+SCALAR_PASSES = 3
+
+FLOPS = 2 * IMAGES * PIXELS * CODEWORDS * CHANNELS
+
+
+def rows_in_copy_order(rows):
+    return rows.rearrange("p c j (q i) -> p c q j i", i=RUN)
+
+
+def words_in_copy_order(words):
+    return words.rearrange("p c (q i) j -> p c q j i", i=RUN)
+
+
+def tile_lvc_pb_k_kernel(tc, assign, xp, codebook, out):
+    nc = tc.nc
+    with ExitStack() as ctx:
+        const = ctx.enter_context(tc.tile_pool(name="const", bufs=1))
+        raw = ctx.enter_context(tc.tile_pool(name="raw", bufs=4))
+        grouped = ctx.enter_context(tc.tile_pool(name="grouped", bufs=3))
+        packed = ctx.enter_context(tc.tile_pool(name="packed", bufs=3))
+        psum = ctx.enter_context(tc.psum_pool(name="psum", bufs=IMAGES))
+        ctx.enter_context(tc.manual_schedule())
+
+        book = const.tile([P, CHANNELS], BF16)
+        nc.scalar.dma_start(out=book[:], in_=codebook)
+        ones = const.tile([P, 1], BF16)
+        nc.vector.memset(ones[:], 1.0)
+        result = const.tile([P, IMAGES, CHANNELS], F32)
+
+        sums = [psum.tile([P, 1], F32, name="sums") for image in range(IMAGES)]
+        acc = [psum.tile([P, CHANNELS], F32, name="acc") for image in range(IMAGES)]
+
+        def load_and_regroup(image, chunk):
+            pixels = slice(chunk * CHUNK_PIXELS, (chunk + 1) * CHUNK_PIXELS)
+            a_rows = raw.tile([P, PASSES, PACK, CODEWORDS], BF16)
+            nc.sync.dma_start(
+                out=a_rows[:],
+                in_=assign[image, pixels, :].rearrange("(c p j) w -> p c j w", p=P, j=PACK),
+            )
+            x_rows = raw.tile([P, PASSES, PACK, CHANNELS], BF16)
+            nc.sync.dma_start(
+                out=x_rows[:],
+                in_=xp[image, pixels, :].rearrange("(c p j) w -> p c j w", p=P, j=PACK),
+            )
+
+            for c in range(PASSES):
+                for j in range(PACK):
+                    nc.tensor.matmul(
+                        out=sums[image][:],
+                        lhsT=a_rows[:, c, j, :],
+                        rhs=ones[:],
+                        start=(chunk == 0 and c == 0 and j == 0),
+                        stop=(chunk == CHUNKS - 1 and c == PASSES - 1 and j == PACK - 1),
+                    )
+
+            a_words = grouped.tile([P, PASSES, CODEWORDS, PACK], BF16, align_bytes=64)
+            x_words = grouped.tile([P, PASSES, CHANNELS, PACK], BF16, align_bytes=64)
+            for c in range(SCALAR_PASSES):
+                nc.scalar.copy(
+                    out=words_in_copy_order(x_words[:, c : c + 1]),
+                    in_=rows_in_copy_order(x_rows[:, c : c + 1]),
+                )
+            nc.vector.tensor_copy(
+                out=words_in_copy_order(a_words[:]), in_=rows_in_copy_order(a_rows[:])
+            )
+            nc.vector.tensor_copy(
+                out=words_in_copy_order(x_words[:, SCALAR_PASSES:]),
+                in_=rows_in_copy_order(x_rows[:, SCALAR_PASSES:]),
+            )
+            return a_words, x_words
+
+        def quantise_and_multiply(image, chunk, a_words, x_words):
+            a_codes = packed.tile([P, PASSES * CODEWORDS], U32, align_bytes=64)
+            a_scales = packed.tile([P, PASSES * CODEWORDS], U8, align_bytes=64)
+            nc.vector.quantize_mx(
+                out=a_codes[:].bitcast(FP8X4),
+                scales=a_scales[:],
+                in_=a_words[:].rearrange("p c w j -> p (c w j)"),
+            )
+            x_codes = packed.tile([P, PASSES * CHANNELS], U32, align_bytes=64)
+            x_scales = packed.tile([P, PASSES * CHANNELS], U8, align_bytes=64)
+            nc.vector.quantize_mx(
+                out=x_codes[:].bitcast(FP8X4),
+                scales=x_scales[:],
+                in_=x_words[:].rearrange("p c w j -> p (c w j)"),
+            )
+            for c in range(PASSES):
+                a_cols = slice(c * CODEWORDS, (c + 1) * CODEWORDS)
+                x_cols = slice(c * CHANNELS, (c + 1) * CHANNELS)
+                nc.tensor.matmul_mx(
+                    out=acc[image][:],
+                    lhsT=a_codes[:, a_cols].bitcast(FP8X4),
+                    lhsT_scale=a_scales[:, a_cols],
+                    rhs=x_codes[:, x_cols].bitcast(FP8X4),
+                    rhs_scale=x_scales[:, x_cols],
+                    start=(chunk == 0 and c == 0),
+                    stop=(chunk == CHUNKS - 1 and c == PASSES - 1),
+                )
+
+        def subtract_codebook(image):
+            minus_sum = const.tile([P, 1], F32, name="minus_sum%d" % image)
+            nc.vector.tensor_scalar_mul(out=minus_sum[:], in0=sums[image][:], scalar1=-1.0)
+            nc.vector.scalar_tensor_tensor(
+                out=result[:, image, :],
+                in0=book[:],
+                scalar=minus_sum[:, 0:1],
+                in1=acc[image][:],
+                op0=MULT,
+                op1=ADD,
+            )
+
+        steps = [(image, chunk) for image in range(IMAGES) for chunk in range(CHUNKS)]
+        words = None
+        for image, chunk in steps:
+            next_words = load_and_regroup(image, chunk)
+            if image > 0 and chunk == 1:
+                subtract_codebook(image - 1)
+            if words is not None:
+                quantise_and_multiply(*words)
+            words = (image, chunk) + next_words
+        quantise_and_multiply(*words)
+        subtract_codebook(IMAGES - 1)
+
+        nc.sync.dma_start(out=out.rearrange("b k c -> k b c"), in_=result[:])

@@ -12,29 +12,41 @@ ADD = mybir.AluOpType.add
 
 P = 128
 PACK = 4
-K_PASS = P * PACK
 
 IMAGES = 2
 PIXELS = 16384
 CODEWORDS = 128
 CHANNELS = 256
 
-PASSES = 4
-CHUNK_PIXELS = PASSES * K_PASS
-CHUNKS = PIXELS // CHUNK_PIXELS
+STRETCHES = P // 2
+QUARTERS = 4
+ROWS = 16
+HALVES = PIXELS // (STRETCHES * QUARTERS * 2 * ROWS)
+PASSES = ROWS // PACK
+
 RUN = 4
 
-SCALAR_PASSES = 3
+SCALAR_COLUMNS = 3 * PASSES * CHANNELS // 4
 
 FLOPS = 2 * IMAGES * PIXELS * CODEWORDS * CHANNELS
 
 
+def chunk_side(tensor, image, half, quarter, side):
+    stretches = tensor[image].rearrange(
+        "(half stretch pixel) w -> half stretch pixel w", half=HALVES, stretch=STRETCHES
+    )
+    first_pixel = (quarter * 2 + side) * ROWS
+    return stretches[half, :, first_pixel : first_pixel + ROWS, :].rearrange(
+        "stretch row w -> stretch (row w)"
+    )
+
+
 def rows_in_copy_order(rows):
-    return rows.rearrange("p c j (q i) -> p c q j i", i=RUN)
+    return rows.rearrange("p t (q i) -> p q t i", i=RUN)
 
 
 def words_in_copy_order(words):
-    return words.rearrange("p c (q i) j -> p c q j i", i=RUN)
+    return words.rearrange("p (q i) t -> p q t i", i=RUN)
 
 
 def tile_lvc_pb_k_kernel(tc, assign, xp, codebook, out):
@@ -56,71 +68,69 @@ def tile_lvc_pb_k_kernel(tc, assign, xp, codebook, out):
         sums = [psum.tile([P, 1], F32, name="sums") for image in range(IMAGES)]
         acc = [psum.tile([P, CHANNELS], F32, name="acc") for image in range(IMAGES)]
 
-        def load_and_regroup(image, chunk):
-            pixels = slice(chunk * CHUNK_PIXELS, (chunk + 1) * CHUNK_PIXELS)
-            a_rows = raw.tile([P, PASSES, PACK, CODEWORDS], BF16)
-            nc.sync.dma_start(
-                out=a_rows[:],
-                in_=assign[image, pixels, :].rearrange("(c p j) w -> p c j w", p=P, j=PACK),
-            )
-            x_rows = raw.tile([P, PASSES, PACK, CHANNELS], BF16)
-            nc.sync.dma_start(
-                out=x_rows[:],
-                in_=xp[image, pixels, :].rearrange("(c p j) w -> p c j w", p=P, j=PACK),
-            )
-
-            for c in range(PASSES):
-                for j in range(PACK):
-                    nc.tensor.matmul(
-                        out=sums[image][:],
-                        lhsT=a_rows[:, c, j, :],
-                        rhs=ones[:],
-                        start=(chunk == 0 and c == 0 and j == 0),
-                        stop=(chunk == CHUNKS - 1 and c == PASSES - 1 and j == PACK - 1),
+        def load_and_regroup(image, half, quarter):
+            first = half == 0 and quarter == 0
+            last = half == HALVES - 1 and quarter == QUARTERS - 1
+            a_rows = raw.tile([P, PACK, PASSES * CODEWORDS], BF16)
+            x_rows = raw.tile([P, PACK, PASSES * CHANNELS], BF16)
+            for rows, tensor in ((a_rows, assign), (x_rows, xp)):
+                for side in range(2):
+                    nc.sync.dma_start(
+                        out=rows[side:P:2].rearrange("p t v -> p (t v)"),
+                        in_=chunk_side(tensor, image, half, quarter, side),
                     )
 
-            a_words = grouped.tile([P, PASSES, CODEWORDS, PACK], BF16, align_bytes=64)
-            x_words = grouped.tile([P, PASSES, CHANNELS, PACK], BF16, align_bytes=64)
-            for c in range(SCALAR_PASSES):
-                nc.scalar.copy(
-                    out=words_in_copy_order(x_words[:, c : c + 1]),
-                    in_=rows_in_copy_order(x_rows[:, c : c + 1]),
-                )
+            for t in range(PACK):
+                for g in range(PASSES):
+                    nc.tensor.matmul(
+                        out=sums[image][:],
+                        lhsT=a_rows[:, t, g * CODEWORDS : (g + 1) * CODEWORDS],
+                        rhs=ones[:],
+                        start=(first and t == 0 and g == 0),
+                        stop=(last and t == PACK - 1 and g == PASSES - 1),
+                    )
+
+            a_words = grouped.tile([P, PASSES * CODEWORDS, PACK], BF16, align_bytes=64)
+            x_words = grouped.tile([P, PASSES * CHANNELS, PACK], BF16, align_bytes=64)
+            nc.scalar.copy(
+                out=words_in_copy_order(x_words[:, :SCALAR_COLUMNS, :]),
+                in_=rows_in_copy_order(x_rows[:, :, :SCALAR_COLUMNS]),
+            )
             nc.vector.tensor_copy(
                 out=words_in_copy_order(a_words[:]), in_=rows_in_copy_order(a_rows[:])
             )
             nc.vector.tensor_copy(
-                out=words_in_copy_order(x_words[:, SCALAR_PASSES:]),
-                in_=rows_in_copy_order(x_rows[:, SCALAR_PASSES:]),
+                out=words_in_copy_order(x_words[:, SCALAR_COLUMNS:, :]),
+                in_=rows_in_copy_order(x_rows[:, :, SCALAR_COLUMNS:]),
             )
-            return a_words, x_words
+            return first, last, a_words, x_words
 
-        def quantise_and_multiply(image, chunk, a_words, x_words):
+        def quantise_and_multiply(image, first, last, a_words, x_words):
             a_codes = packed.tile([P, PASSES * CODEWORDS], U32, align_bytes=64)
             a_scales = packed.tile([P, PASSES * CODEWORDS], U8, align_bytes=64)
             nc.vector.quantize_mx(
                 out=a_codes[:].bitcast(FP8X4),
                 scales=a_scales[:],
-                in_=a_words[:].rearrange("p c w j -> p (c w j)"),
+                in_=a_words[:].rearrange("p v t -> p (v t)"),
             )
             x_codes = packed.tile([P, PASSES * CHANNELS], U32, align_bytes=64)
             x_scales = packed.tile([P, PASSES * CHANNELS], U8, align_bytes=64)
             nc.vector.quantize_mx(
                 out=x_codes[:].bitcast(FP8X4),
                 scales=x_scales[:],
-                in_=x_words[:].rearrange("p c w j -> p (c w j)"),
+                in_=x_words[:].rearrange("p v t -> p (v t)"),
             )
-            for c in range(PASSES):
-                a_cols = slice(c * CODEWORDS, (c + 1) * CODEWORDS)
-                x_cols = slice(c * CHANNELS, (c + 1) * CHANNELS)
+            for g in range(PASSES):
+                a_cols = slice(g * CODEWORDS, (g + 1) * CODEWORDS)
+                x_cols = slice(g * CHANNELS, (g + 1) * CHANNELS)
                 nc.tensor.matmul_mx(
                     out=acc[image][:],
                     lhsT=a_codes[:, a_cols].bitcast(FP8X4),
                     lhsT_scale=a_scales[:, a_cols],
                     rhs=x_codes[:, x_cols].bitcast(FP8X4),
                     rhs_scale=x_scales[:, x_cols],
-                    start=(chunk == 0 and c == 0),
-                    stop=(chunk == CHUNKS - 1 and c == PASSES - 1),
+                    start=(first and g == 0),
+                    stop=(last and g == PASSES - 1),
                 )
 
         def subtract_codebook(image):
@@ -135,15 +145,20 @@ def tile_lvc_pb_k_kernel(tc, assign, xp, codebook, out):
                 op1=ADD,
             )
 
-        steps = [(image, chunk) for image in range(IMAGES) for chunk in range(CHUNKS)]
+        chunks = [
+            (image, half, quarter)
+            for image in range(IMAGES)
+            for half in range(HALVES)
+            for quarter in range(QUARTERS)
+        ]
         words = None
-        for image, chunk in steps:
-            next_words = load_and_regroup(image, chunk)
-            if image > 0 and chunk == 1:
+        for image, half, quarter in chunks:
+            next_words = load_and_regroup(image, half, quarter)
+            if image > 0 and half == 0 and quarter == 1:
                 subtract_codebook(image - 1)
             if words is not None:
                 quantise_and_multiply(*words)
-            words = (image, chunk) + next_words
+            words = (image,) + next_words
         quantise_and_multiply(*words)
         subtract_codebook(IMAGES - 1)
 

@@ -24,7 +24,7 @@ ROWS = 16
 HALVES = PIXELS // (STRETCHES * QUARTERS * 2 * ROWS)
 PASSES = ROWS // PACK
 
-RUN = 4
+RUN = 8
 
 SCALAR_COLUMNS = 3 * PASSES * CHANNELS // 4
 

@@ -22,40 +22,89 @@ STRETCHES = P // 2
 QUARTERS = 4
 ROWS = 16
 HALVES = PIXELS // (STRETCHES * QUARTERS * 2 * ROWS)
-PASSES = ROWS // PACK
+CHUNK_PASSES = ROWS // PACK
+
+HEAD = (2, 2)
+TAIL = (2, 1, 1)
 
 RUN = 8
 
-SCALAR_COLUMNS = 3 * PASSES * CHANNELS // 4
+SCALAR_CHANNELS = 192
+TAIL_SCALAR_CHANNELS = 160
 
 FLOPS = 2 * IMAGES * PIXELS * CODEWORDS * CHANNELS
 
 
-def chunk_side(tensor, image, half, quarter, side):
+def side_of(tensor, image, half, first_quarter, quarters, first_row, rows, side):
     stretches = tensor[image].rearrange(
-        "(half stretch pixel) w -> half stretch pixel w", half=HALVES, stretch=STRETCHES
+        "(half stretch quarter side row) w -> half stretch quarter side row w",
+        half=HALVES,
+        stretch=STRETCHES,
+        quarter=QUARTERS,
+        side=2,
     )
-    first_pixel = (quarter * 2 + side) * ROWS
-    return stretches[half, :, first_pixel : first_pixel + ROWS, :].rearrange(
-        "stretch row w -> stretch (row w)"
-    )
+    return stretches[
+        half,
+        :,
+        first_quarter : first_quarter + quarters,
+        side,
+        first_row : first_row + rows,
+        :,
+    ].rearrange("stretch quarter row w -> stretch quarter (row w)")
+
+
+def xp_pieces():
+    chunks = [
+        (image, half, quarter)
+        for image in range(IMAGES)
+        for half in range(HALVES)
+        for quarter in range(QUARTERS)
+    ]
+    pieces = []
+    for chunk in chunks:
+        cuts = (CHUNK_PASSES,)
+        if chunk == chunks[0]:
+            cuts = HEAD
+        if chunk == chunks[-1]:
+            cuts = TAIL
+        first_row = 0
+        for passes in cuts:
+            pieces.append(chunk + (first_row, passes))
+            first_row += passes * PACK
+    return pieces
+
+
+def assign_groups():
+    groups = []
+    for image in range(IMAGES):
+        for half in range(HALVES):
+            for quarter in range(0, QUARTERS, 2):
+                if image == 0 and half == 0 and quarter == 0:
+                    groups.append((image, half, 0, 1))
+                    groups.append((image, half, 1, 1))
+                else:
+                    groups.append((image, half, quarter, 2))
+    return groups
 
 
 def rows_in_copy_order(rows):
-    return rows.rearrange("p t (q i) -> p q t i", i=RUN)
+    return rows.rearrange("p g t (q i) -> p g q t i", i=RUN)
 
 
 def words_in_copy_order(words):
-    return words.rearrange("p (q i) t -> p q t i", i=RUN)
+    return words.rearrange("p g (q i) t -> p g q t i", i=RUN)
 
 
 def tile_lvc_pb_k_kernel(tc, assign, xp, codebook, out):
     nc = tc.nc
     with ExitStack() as ctx:
         const = ctx.enter_context(tc.tile_pool(name="const", bufs=1))
-        raw = ctx.enter_context(tc.tile_pool(name="raw", bufs=4))
-        grouped = ctx.enter_context(tc.tile_pool(name="grouped", bufs=3))
-        packed = ctx.enter_context(tc.tile_pool(name="packed", bufs=3))
+        raw_a = ctx.enter_context(tc.tile_pool(name="raw_a", bufs=3))
+        raw_x = ctx.enter_context(tc.tile_pool(name="raw_x", bufs=7))
+        grouped_a = ctx.enter_context(tc.tile_pool(name="grouped_a", bufs=2))
+        grouped_x = ctx.enter_context(tc.tile_pool(name="grouped_x", bufs=4))
+        packed_a = ctx.enter_context(tc.tile_pool(name="packed_a", bufs=4))
+        packed_x = ctx.enter_context(tc.tile_pool(name="packed_x", bufs=8))
         psum = ctx.enter_context(tc.psum_pool(name="psum", bufs=IMAGES))
         ctx.enter_context(tc.manual_schedule())
 
@@ -63,65 +112,119 @@ def tile_lvc_pb_k_kernel(tc, assign, xp, codebook, out):
         nc.scalar.dma_start(out=book[:], in_=codebook)
         ones = const.tile([P, 1], BF16)
         nc.vector.memset(ones[:], 1.0)
-        result = const.tile([P, IMAGES, CHANNELS], F32)
 
         sums = [psum.tile([P, 1], F32, name="sums") for image in range(IMAGES)]
         acc = [psum.tile([P, CHANNELS], F32, name="acc") for image in range(IMAGES)]
 
-        def load_and_regroup(image, half, quarter):
-            first = half == 0 and quarter == 0
-            last = half == HALVES - 1 and quarter == QUARTERS - 1
-            a_rows = raw.tile([P, PACK, PASSES * CODEWORDS], BF16)
-            x_rows = raw.tile([P, PACK, PASSES * CHANNELS], BF16)
-            for rows, tensor in ((a_rows, assign), (x_rows, xp)):
-                for side in range(2):
-                    nc.sync.dma_start(
-                        out=rows[side:P:2].rearrange("p t v -> p (t v)"),
-                        in_=chunk_side(tensor, image, half, quarter, side),
-                    )
+        pieces = xp_pieces()
+        groups = assign_groups()
+        group_of = {}
+        for number, (image, half, first_quarter, quarters) in enumerate(groups):
+            for quarter in range(first_quarter, first_quarter + quarters):
+                group_of[(image, half, quarter)] = number
+        needed_by = [
+            min(i for i, piece in enumerate(pieces) if group_of[piece[:3]] == number)
+            for number in range(len(groups))
+        ]
 
-            for t in range(PACK):
-                for g in range(PASSES):
-                    nc.tensor.matmul(
-                        out=sums[image][:],
-                        lhsT=a_rows[:, t, g * CODEWORDS : (g + 1) * CODEWORDS],
-                        rhs=ones[:],
-                        start=(first and t == 0 and g == 0),
-                        stop=(last and t == PACK - 1 and g == PASSES - 1),
-                    )
+        a_rows_of, x_rows_of = {}, {}
+        a_words_of, x_words_of = {}, {}
+        a_packed_of = {}
 
-            a_words = grouped.tile([P, PASSES * CODEWORDS, PACK], BF16, align_bytes=64)
-            x_words = grouped.tile([P, PASSES * CHANNELS, PACK], BF16, align_bytes=64)
+        def load_assign(number):
+            image, half, first_quarter, quarters = groups[number]
+            a_rows = raw_a.tile([P, quarters * CHUNK_PASSES, PACK, CODEWORDS], BF16)
+            for side in range(2):
+                nc.sync.dma_start(
+                    out=a_rows[side:P:2].rearrange("p (h g) t w -> p h (g t w)", h=quarters),
+                    in_=side_of(assign, image, half, first_quarter, quarters, 0, ROWS, side),
+                )
+            a_rows_of[number] = a_rows
+
+        def load_xp(i):
+            image, half, quarter, first_row, passes = pieces[i]
+            x_rows = raw_x.tile([P, passes, PACK, CHANNELS], BF16)
+            for side in range(2):
+                nc.sync.dma_start(
+                    out=x_rows[side:P:2].rearrange("p (h g) t w -> p h (g t w)", h=1),
+                    in_=side_of(xp, image, half, quarter, 1, first_row, passes * PACK, side),
+                )
+            x_rows_of[i] = x_rows
+
+        def sum_assign(number):
+            image, half, first_quarter, quarters = groups[number]
+            opens = half == 0 and first_quarter == 0
+            closes = half == HALVES - 1 and first_quarter + quarters == QUARTERS
+            rows = [(g, t) for g in range(quarters * CHUNK_PASSES) for t in range(PACK)]
+            for row in rows:
+                nc.tensor.matmul(
+                    out=sums[image][:],
+                    lhsT=a_rows_of[number][:, row[0], row[1], :],
+                    rhs=ones[:],
+                    start=(opens and row == rows[0]),
+                    stop=(closes and row == rows[-1]),
+                )
+
+        def regroup_assign(number):
+            passes = groups[number][3] * CHUNK_PASSES
+            a_words = grouped_a.tile([P, passes, CODEWORDS, PACK], BF16, align_bytes=64)
+            nc.vector.tensor_copy(
+                out=words_in_copy_order(a_words[:]),
+                in_=rows_in_copy_order(a_rows_of[number][:]),
+            )
+            a_words_of[number] = a_words
+
+        def regroup_xp(i):
+            passes = pieces[i][4]
+            share = SCALAR_CHANNELS
+            if pieces[i][:3] == pieces[-1][:3]:
+                share = TAIL_SCALAR_CHANNELS
+            x_words = grouped_x.tile([P, passes, CHANNELS, PACK], BF16, align_bytes=64)
             nc.scalar.copy(
-                out=words_in_copy_order(x_words[:, :SCALAR_COLUMNS, :]),
-                in_=rows_in_copy_order(x_rows[:, :, :SCALAR_COLUMNS]),
+                out=words_in_copy_order(x_words[:, :, :share, :]),
+                in_=rows_in_copy_order(x_rows_of[i][:, :, :, :share]),
             )
             nc.vector.tensor_copy(
-                out=words_in_copy_order(a_words[:]), in_=rows_in_copy_order(a_rows[:])
+                out=words_in_copy_order(x_words[:, :, share:, :]),
+                in_=rows_in_copy_order(x_rows_of[i][:, :, :, share:]),
             )
-            nc.vector.tensor_copy(
-                out=words_in_copy_order(x_words[:, SCALAR_COLUMNS:, :]),
-                in_=rows_in_copy_order(x_rows[:, :, SCALAR_COLUMNS:]),
-            )
-            return first, last, a_words, x_words
+            x_words_of[i] = x_words
 
-        def quantise_and_multiply(image, first, last, a_words, x_words):
-            a_codes = packed.tile([P, PASSES * CODEWORDS], U32, align_bytes=64)
-            a_scales = packed.tile([P, PASSES * CODEWORDS], U8, align_bytes=64)
+        def quantise_assign(number):
+            passes = groups[number][3] * CHUNK_PASSES
+            a_codes = packed_a.tile([P, passes * CODEWORDS], U32, align_bytes=64)
+            a_scales = packed_a.tile([P, passes * CODEWORDS], U8, align_bytes=64)
             nc.vector.quantize_mx(
                 out=a_codes[:].bitcast(FP8X4),
                 scales=a_scales[:],
-                in_=a_words[:].rearrange("p v t -> p (v t)"),
+                in_=a_words_of[number][:].rearrange("p g v t -> p (g v t)"),
             )
-            x_codes = packed.tile([P, PASSES * CHANNELS], U32, align_bytes=64)
-            x_scales = packed.tile([P, PASSES * CHANNELS], U8, align_bytes=64)
+            a_packed_of[number] = (a_codes, a_scales)
+
+        def quantise_xp(i):
+            passes = pieces[i][4]
+            x_codes = packed_x.tile([P, passes * CHANNELS], U32, align_bytes=64)
+            x_scales = packed_x.tile([P, passes * CHANNELS], U8, align_bytes=64)
             nc.vector.quantize_mx(
                 out=x_codes[:].bitcast(FP8X4),
                 scales=x_scales[:],
-                in_=x_words[:].rearrange("p v t -> p (v t)"),
+                in_=x_words_of[i][:].rearrange("p g v t -> p (g v t)"),
             )
-            for g in range(PASSES):
-                a_cols = slice(g * CODEWORDS, (g + 1) * CODEWORDS)
+            return x_codes, x_scales
+
+        def multiply(i, x_codes, x_scales):
+            image, half, quarter, first_row, passes = pieces[i]
+            number = group_of[(image, half, quarter)]
+            a_codes, a_scales = a_packed_of[number]
+            before = (quarter - groups[number][2]) * CHUNK_PASSES + first_row // PACK
+            opens = half == 0 and quarter == 0 and first_row == 0
+            closes = (
+                half == HALVES - 1
+                and quarter == QUARTERS - 1
+                and first_row + passes * PACK == ROWS
+            )
+            for g in range(passes):
+                a_cols = slice((before + g) * CODEWORDS, (before + g + 1) * CODEWORDS)
                 x_cols = slice(g * CHANNELS, (g + 1) * CHANNELS)
                 nc.tensor.matmul_mx(
                     out=acc[image][:],
@@ -129,37 +232,46 @@ def tile_lvc_pb_k_kernel(tc, assign, xp, codebook, out):
                     lhsT_scale=a_scales[:, a_cols],
                     rhs=x_codes[:, x_cols].bitcast(FP8X4),
                     rhs_scale=x_scales[:, x_cols],
-                    start=(first and g == 0),
-                    stop=(last and g == PASSES - 1),
+                    start=(opens and g == 0),
+                    stop=(closes and g == passes - 1),
                 )
 
         def subtract_codebook(image):
             minus_sum = const.tile([P, 1], F32, name="minus_sum%d" % image)
+            result = const.tile([P, CHANNELS], F32, name="result%d" % image)
             nc.vector.tensor_scalar_mul(out=minus_sum[:], in0=sums[image][:], scalar1=-1.0)
             nc.vector.scalar_tensor_tensor(
-                out=result[:, image, :],
+                out=result[:],
                 in0=book[:],
                 scalar=minus_sum[:, 0:1],
                 in1=acc[image][:],
                 op0=MULT,
                 op1=ADD,
             )
+            return result
 
-        chunks = [
-            (image, half, quarter)
-            for image in range(IMAGES)
-            for half in range(HALVES)
-            for quarter in range(QUARTERS)
-        ]
-        words = None
-        for image, half, quarter in chunks:
-            next_words = load_and_regroup(image, half, quarter)
-            if image > 0 and half == 0 and quarter == 1:
-                subtract_codebook(image - 1)
-            if words is not None:
-                quantise_and_multiply(*words)
-            words = (image,) + next_words
-        quantise_and_multiply(*words)
-        subtract_codebook(IMAGES - 1)
+        results = []
+        for i in range(len(pieces) + 1):
+            new_groups = [number for number, piece in enumerate(needed_by) if piece == i]
+            if i == 0:
+                load_xp(i)
+            for number in new_groups:
+                load_assign(number)
+                sum_assign(number)
+                regroup_assign(number)
+            if 0 < i < len(pieces):
+                load_xp(i)
+            if i < len(pieces):
+                regroup_xp(i)
+            if i > 0:
+                if len(results) < pieces[i - 1][0] and needed_by[group_of[pieces[i - 1][:3]]] < i - 1:
+                    results.append(subtract_codebook(pieces[i - 1][0] - 1))
+                packed = quantise_xp(i - 1)
+            for number in new_groups:
+                quantise_assign(number)
+            if i > 0:
+                multiply(i - 1, *packed)
+        results.append(subtract_codebook(IMAGES - 1))
 
-        nc.sync.dma_start(out=out.rearrange("b k c -> k b c"), in_=result[:])
+        for image in range(IMAGES):
+            nc.sync.dma_start(out=out[image], in_=results[image][:])

@@ -1,6 +1,7 @@
 from contextlib import ExitStack
 
 import concourse.mybir as mybir
+from concourse.masks import make_identity
 
 BF16 = mybir.dt.bfloat16
 F32 = mybir.dt.float32
@@ -29,8 +30,11 @@ TAIL = (2, 1, 1)
 
 RUN = 8
 
-SCALAR_CHANNELS = 192
-TAIL_SCALAR_CHANNELS = 160
+SCALAR_CHANNELS = (136, 256)
+TAIL_SCALAR_CHANNELS = 152
+
+MOVED_CHANNELS = 56
+MOVED_PASSES = 2
 
 FLOPS = 2 * IMAGES * PIXELS * CODEWORDS * CHANNELS
 
@@ -106,12 +110,15 @@ def tile_lvc_pb_k_kernel(tc, assign, xp, codebook, out):
         packed_a = ctx.enter_context(tc.tile_pool(name="packed_a", bufs=4))
         packed_x = ctx.enter_context(tc.tile_pool(name="packed_x", bufs=8))
         psum = ctx.enter_context(tc.psum_pool(name="psum", bufs=IMAGES))
+        psum_moved = ctx.enter_context(tc.psum_pool(name="psum_moved", bufs=3))
         ctx.enter_context(tc.manual_schedule())
 
         book = const.tile([P, CHANNELS], BF16)
         nc.scalar.dma_start(out=book[:], in_=codebook)
         ones = const.tile([P, 1], BF16)
         nc.vector.memset(ones[:], 1.0)
+        identity = const.tile([P, P], BF16)
+        make_identity(nc, identity[:])
 
         sums = [psum.tile([P, 1], F32, name="sums") for image in range(IMAGES)]
         acc = [psum.tile([P, CHANNELS], F32, name="acc") for image in range(IMAGES)]
@@ -176,18 +183,37 @@ def tile_lvc_pb_k_kernel(tc, assign, xp, codebook, out):
 
         def regroup_xp(i):
             passes = pieces[i][4]
-            share = SCALAR_CHANNELS
+            share = SCALAR_CHANNELS[pieces[i][2] % 2]
             if pieces[i][:3] == pieces[-1][:3]:
                 share = TAIL_SCALAR_CHANNELS
             x_words = grouped_x.tile([P, passes, CHANNELS, PACK], BF16, align_bytes=64)
+            own = share
+            if share == CHANNELS:
+                own = CHANNELS - MOVED_CHANNELS
+                moved = psum_moved.tile([P, passes, MOVED_CHANNELS * PACK], BF16)
+                for g in range(0, passes, MOVED_PASSES):
+                    these = slice(g, g + MOVED_PASSES)
+                    nc.tensor.matmul(
+                        out=moved[:, these, :].rearrange("p g v -> p (g v)"),
+                        lhsT=identity[:],
+                        rhs=x_rows_of[i][:, these, :, own:].rearrange("p g t c -> p g c t"),
+                        start=True,
+                        stop=True,
+                    )
             nc.scalar.copy(
-                out=words_in_copy_order(x_words[:, :, :share, :]),
-                in_=rows_in_copy_order(x_rows_of[i][:, :, :, :share]),
+                out=words_in_copy_order(x_words[:, :, :own, :]),
+                in_=rows_in_copy_order(x_rows_of[i][:, :, :, :own]),
             )
-            nc.vector.tensor_copy(
-                out=words_in_copy_order(x_words[:, :, share:, :]),
-                in_=rows_in_copy_order(x_rows_of[i][:, :, :, share:]),
-            )
+            if own < share:
+                nc.scalar.copy(
+                    out=x_words[:, :, own:, :].rearrange("p g c t -> p g (c t)"),
+                    in_=moved[:],
+                )
+            if share < CHANNELS:
+                nc.vector.tensor_copy(
+                    out=words_in_copy_order(x_words[:, :, share:, :]),
+                    in_=rows_in_copy_order(x_rows_of[i][:, :, :, share:]),
+                )
             x_words_of[i] = x_words
 
         def quantise_assign(number):

@@ -30,8 +30,8 @@ TAIL = (2, 1, 1)
 
 RUN = 8
 
-SCALAR_CHANNELS = (136, 256)
-TAIL_SCALAR_CHANNELS = 152
+SCALAR_CHANNELS = (152, 256)
+TAIL_SCALAR_CHANNELS = 160
 
 MOVED_CHANNELS = 56
 MOVED_PASSES = 2
@@ -281,13 +281,13 @@ def tile_lvc_pb_k_kernel(tc, assign, xp, codebook, out):
             new_groups = [number for number, piece in enumerate(needed_by) if piece == i]
             if i == 0:
                 load_xp(i)
+                regroup_xp(i)
             for number in new_groups:
                 load_assign(number)
                 sum_assign(number)
                 regroup_assign(number)
             if 0 < i < len(pieces):
                 load_xp(i)
-            if i < len(pieces):
                 regroup_xp(i)
             if i > 0:
                 if len(results) < pieces[i - 1][0] and needed_by[group_of[pieces[i - 1][:3]]] < i - 1:

@@ -30,8 +30,8 @@ TAIL = (2, 1, 1)
 
 RUN = 8
 
-SCALAR_CHANNELS = (152, 256)
-TAIL_SCALAR_CHANNELS = 160
+SCALAR_CHANNELS = (160, 256)
+TAIL_SCALAR_CHANNELS = 176
 
 MOVED_CHANNELS = 56
 MOVED_PASSES = 2
@@ -83,11 +83,7 @@ def assign_groups():
     for image in range(IMAGES):
         for half in range(HALVES):
             for quarter in range(0, QUARTERS, 2):
-                if image == 0 and half == 0 and quarter == 0:
-                    groups.append((image, half, 0, 1))
-                    groups.append((image, half, 1, 1))
-                else:
-                    groups.append((image, half, quarter, 2))
+                groups.append((image, half, quarter, 2))
     return groups
 
 

from contextlib import ExitStack

import concourse.mybir as mybir
from concourse.masks import make_identity

BF16 = mybir.dt.bfloat16
F32 = mybir.dt.float32
U32 = mybir.dt.uint32
U8 = mybir.dt.uint8
FP8X4 = mybir.dt.float8_e4m3fn_x4
MULT = mybir.AluOpType.mult
ADD = mybir.AluOpType.add

P = 128
PACK = 4

IMAGES = 2
PIXELS = 16384
CODEWORDS = 128
CHANNELS = 256

STRETCHES = P // 2
QUARTERS = 4
ROWS = 16
HALVES = PIXELS // (STRETCHES * QUARTERS * 2 * ROWS)
CHUNK_PASSES = ROWS // PACK

HEAD = (2, 2)
TAIL = (2, 1, 1)

RUN = 8

SCALAR_CHANNELS = (160, 256)
TAIL_SCALAR_CHANNELS = 176

MOVED_CHANNELS = 56
MOVED_PASSES = 2

FLOPS = 2 * IMAGES * PIXELS * CODEWORDS * CHANNELS


def side_of(tensor, image, half, first_quarter, quarters, first_row, rows, side):
    stretches = tensor[image].rearrange(
        "(half stretch quarter side row) w -> half stretch quarter side row w",
        half=HALVES,
        stretch=STRETCHES,
        quarter=QUARTERS,
        side=2,
    )
    return stretches[
        half,
        :,
        first_quarter : first_quarter + quarters,
        side,
        first_row : first_row + rows,
        :,
    ].rearrange("stretch quarter row w -> stretch quarter (row w)")


def xp_pieces():
    chunks = [
        (image, half, quarter)
        for image in range(IMAGES)
        for half in range(HALVES)
        for quarter in range(QUARTERS)
    ]
    pieces = []
    for chunk in chunks:
        cuts = (CHUNK_PASSES,)
        if chunk == chunks[0]:
            cuts = HEAD
        if chunk == chunks[-1]:
            cuts = TAIL
        first_row = 0
        for passes in cuts:
            pieces.append(chunk + (first_row, passes))
            first_row += passes * PACK
    return pieces


def assign_groups():
    groups = []
    for image in range(IMAGES):
        for half in range(HALVES):
            for quarter in range(0, QUARTERS, 2):
                groups.append((image, half, quarter, 2))
    return groups


def rows_in_copy_order(rows):
    return rows.rearrange("p g t (q i) -> p g q t i", i=RUN)


def words_in_copy_order(words):
    return words.rearrange("p g (q i) t -> p g q t i", i=RUN)


def tile_lvc_pb_k_kernel(tc, assign, xp, codebook, out):
    nc = tc.nc
    with ExitStack() as ctx:
        const = ctx.enter_context(tc.tile_pool(name="const", bufs=1))
        raw_a = ctx.enter_context(tc.tile_pool(name="raw_a", bufs=3))
        raw_x = ctx.enter_context(tc.tile_pool(name="raw_x", bufs=7))
        grouped_a = ctx.enter_context(tc.tile_pool(name="grouped_a", bufs=2))
        grouped_x = ctx.enter_context(tc.tile_pool(name="grouped_x", bufs=4))
        packed_a = ctx.enter_context(tc.tile_pool(name="packed_a", bufs=4))
        packed_x = ctx.enter_context(tc.tile_pool(name="packed_x", bufs=8))
        psum = ctx.enter_context(tc.psum_pool(name="psum", bufs=IMAGES))
        psum_moved = ctx.enter_context(tc.psum_pool(name="psum_moved", bufs=3))
        ctx.enter_context(tc.manual_schedule())

        book = const.tile([P, CHANNELS], BF16)
        nc.scalar.dma_start(out=book[:], in_=codebook)
        ones = const.tile([P, 1], BF16)
        nc.vector.memset(ones[:], 1.0)
        identity = const.tile([P, P], BF16)
        make_identity(nc, identity[:])

        sums = [psum.tile([P, 1], F32, name="sums") for image in range(IMAGES)]
        acc = [psum.tile([P, CHANNELS], F32, name="acc") for image in range(IMAGES)]

        pieces = xp_pieces()
        groups = assign_groups()
        group_of = {}
        for number, (image, half, first_quarter, quarters) in enumerate(groups):
            for quarter in range(first_quarter, first_quarter + quarters):
                group_of[(image, half, quarter)] = number
        needed_by = [
            min(i for i, piece in enumerate(pieces) if group_of[piece[:3]] == number)
            for number in range(len(groups))
        ]

        a_rows_of, x_rows_of = {}, {}
        a_words_of, x_words_of = {}, {}
        a_packed_of = {}

        def load_assign(number):
            image, half, first_quarter, quarters = groups[number]
            a_rows = raw_a.tile([P, quarters * CHUNK_PASSES, PACK, CODEWORDS], BF16)
            for side in range(2):
                nc.sync.dma_start(
                    out=a_rows[side:P:2].rearrange("p (h g) t w -> p h (g t w)", h=quarters),
                    in_=side_of(assign, image, half, first_quarter, quarters, 0, ROWS, side),
                )
            a_rows_of[number] = a_rows

        def load_xp(i):
            image, half, quarter, first_row, passes = pieces[i]
            x_rows = raw_x.tile([P, passes, PACK, CHANNELS], BF16)
            for side in range(2):
                nc.sync.dma_start(
                    out=x_rows[side:P:2].rearrange("p (h g) t w -> p h (g t w)", h=1),
                    in_=side_of(xp, image, half, quarter, 1, first_row, passes * PACK, side),
                )
            x_rows_of[i] = x_rows

        def sum_assign(number):
            image, half, first_quarter, quarters = groups[number]
            opens = half == 0 and first_quarter == 0
            closes = half == HALVES - 1 and first_quarter + quarters == QUARTERS
            rows = [(g, t) for g in range(quarters * CHUNK_PASSES) for t in range(PACK)]
            for row in rows:
                nc.tensor.matmul(
                    out=sums[image][:],
                    lhsT=a_rows_of[number][:, row[0], row[1], :],
                    rhs=ones[:],
                    start=(opens and row == rows[0]),
                    stop=(closes and row == rows[-1]),
                )

        def regroup_assign(number):
            passes = groups[number][3] * CHUNK_PASSES
            a_words = grouped_a.tile([P, passes, CODEWORDS, PACK], BF16, align_bytes=64)
            nc.vector.tensor_copy(
                out=words_in_copy_order(a_words[:]),
                in_=rows_in_copy_order(a_rows_of[number][:]),
            )
            a_words_of[number] = a_words

        def regroup_xp(i):
            passes = pieces[i][4]
            share = SCALAR_CHANNELS[pieces[i][2] % 2]
            if pieces[i][:3] == pieces[-1][:3]:
                share = TAIL_SCALAR_CHANNELS
            x_words = grouped_x.tile([P, passes, CHANNELS, PACK], BF16, align_bytes=64)
            own = share
            if share == CHANNELS:
                own = CHANNELS - MOVED_CHANNELS
                moved = psum_moved.tile([P, passes, MOVED_CHANNELS * PACK], BF16)
                for g in range(0, passes, MOVED_PASSES):
                    these = slice(g, g + MOVED_PASSES)
                    nc.tensor.matmul(
                        out=moved[:, these, :].rearrange("p g v -> p (g v)"),
                        lhsT=identity[:],
                        rhs=x_rows_of[i][:, these, :, own:].rearrange("p g t c -> p g c t"),
                        start=True,
                        stop=True,
                    )
            nc.scalar.copy(
                out=words_in_copy_order(x_words[:, :, :own, :]),
                in_=rows_in_copy_order(x_rows_of[i][:, :, :, :own]),
            )
            if own < share:
                nc.scalar.copy(
                    out=x_words[:, :, own:, :].rearrange("p g c t -> p g (c t)"),
                    in_=moved[:],
                )
            if share < CHANNELS:
                nc.vector.tensor_copy(
                    out=words_in_copy_order(x_words[:, :, share:, :]),
                    in_=rows_in_copy_order(x_rows_of[i][:, :, :, share:]),
                )
            x_words_of[i] = x_words

        def quantise_assign(number):
            passes = groups[number][3] * CHUNK_PASSES
            a_codes = packed_a.tile([P, passes * CODEWORDS], U32, align_bytes=64)
            a_scales = packed_a.tile([P, passes * CODEWORDS], U8, align_bytes=64)
            nc.vector.quantize_mx(
                out=a_codes[:].bitcast(FP8X4),
                scales=a_scales[:],
                in_=a_words_of[number][:].rearrange("p g v t -> p (g v t)"),
            )
            a_packed_of[number] = (a_codes, a_scales)

        def quantise_xp(i):
            passes = pieces[i][4]
            x_codes = packed_x.tile([P, passes * CHANNELS], U32, align_bytes=64)
            x_scales = packed_x.tile([P, passes * CHANNELS], U8, align_bytes=64)
            nc.vector.quantize_mx(
                out=x_codes[:].bitcast(FP8X4),
                scales=x_scales[:],
                in_=x_words_of[i][:].rearrange("p g v t -> p (g v t)"),
            )
            return x_codes, x_scales

        def multiply(i, x_codes, x_scales):
            image, half, quarter, first_row, passes = pieces[i]
            number = group_of[(image, half, quarter)]
            a_codes, a_scales = a_packed_of[number]
            before = (quarter - groups[number][2]) * CHUNK_PASSES + first_row // PACK
            opens = half == 0 and quarter == 0 and first_row == 0
            closes = (
                half == HALVES - 1
                and quarter == QUARTERS - 1
                and first_row + passes * PACK == ROWS
            )
            for g in range(passes):
                a_cols = slice((before + g) * CODEWORDS, (before + g + 1) * CODEWORDS)
                x_cols = slice(g * CHANNELS, (g + 1) * CHANNELS)
                nc.tensor.matmul_mx(
                    out=acc[image][:],
                    lhsT=a_codes[:, a_cols].bitcast(FP8X4),
                    lhsT_scale=a_scales[:, a_cols],
                    rhs=x_codes[:, x_cols].bitcast(FP8X4),
                    rhs_scale=x_scales[:, x_cols],
                    start=(opens and g == 0),
                    stop=(closes and g == passes - 1),
                )

        def subtract_codebook(image):
            minus_sum = const.tile([P, 1], F32, name="minus_sum%d" % image)
            result = const.tile([P, CHANNELS], F32, name="result%d" % image)
            nc.vector.tensor_scalar_mul(out=minus_sum[:], in0=sums[image][:], scalar1=-1.0)
            nc.vector.scalar_tensor_tensor(
                out=result[:],
                in0=book[:],
                scalar=minus_sum[:, 0:1],
                in1=acc[image][:],
                op0=MULT,
                op1=ADD,
            )
            return result

        results = []
        for i in range(len(pieces) + 1):
            new_groups = [number for number, piece in enumerate(needed_by) if piece == i]
            if i == 0:
                load_xp(i)
                regroup_xp(i)
            for number in new_groups:
                load_assign(number)
                sum_assign(number)
                regroup_assign(number)
            if 0 < i < len(pieces):
                load_xp(i)
                regroup_xp(i)
            if i > 0:
                if len(results) < pieces[i - 1][0] and needed_by[group_of[pieces[i - 1][:3]]] < i - 1:
                    results.append(subtract_codebook(pieces[i - 1][0] - 1))
                packed = quantise_xp(i - 1)
            for number in new_groups:
                quantise_assign(number)
            if i > 0:
                multiply(i - 1, *packed)
        results.append(subtract_codebook(IMAGES - 1))

        for image in range(IMAGES):
            nc.sync.dma_start(out=out[image], in_=results[image][:])
